import numpy as np
import ml_dtypes


def mxq(x, axis, fmt="e4m3"):
    dtype, down = {"e4m3": (ml_dtypes.float8_e4m3fn, 7), "e5m2": (ml_dtypes.float8_e5m2, 14)}[fmt]
    v = np.moveaxis(np.asarray(x, np.float32).astype(ml_dtypes.bfloat16).astype(np.float64), axis, -1)
    blocks = v.reshape(v.shape[:-1] + (-1, 32))
    amax = np.abs(blocks).max(-1, keepdims=True)
    byte = np.maximum(np.where(amax > 0, np.frexp(amax)[1] - 1 + 127, 0) - down, 1)
    scale = np.exp2(byte - 127.0)
    codes = (blocks / scale).astype(np.float32).astype(dtype).astype(np.float64)
    return np.moveaxis((codes * scale).reshape(v.shape), -1, axis)


WIDE = False


def mx_kscale(k):
    if not WIDE:
        return np.ones(k)
    levels = np.array([10, -10, 5, -5, 0])
    if k % 512:
        return np.exp2(np.random.permutation(np.resize(levels, k // 32))).repeat(32)
    a = np.empty((k // 512, 16))
    for p in range(k // 512):
        a[p, :8] = np.random.permutation(np.resize(levels, 8))
        for g in range(8):
            far = levels[np.abs(levels - a[p, g]) >= 10]
            a[p, g + 8] = far[np.random.randint(len(far))]
    return np.exp2(a.ravel()).repeat(32)


BF16 = ml_dtypes.bfloat16


def bf(x):
    return np.asarray(x, np.float32).astype(BF16)


def f64(x):
    return np.asarray(x).astype(np.float64)


B, C, NP, P, HID = 32, 3, 8, 32, 512
IN_D = C * P * P
SEQ = NP * NP + 1
IMG = NP * P


def positional_embedding(seq_len, dim):
    i = np.arange(seq_len)[:, None].astype(np.float64)
    j = np.arange(dim)[None, :].astype(np.float64)
    ang = i / np.power(100000.0, j / dim)
    return np.where(j % 2 == 0, np.sin(ang), np.cos(ang))


def setup_inputs():
    s = mx_kscale(IN_D)
    X = np.random.standard_normal((B, C, NP, P, NP, P)) * s.reshape(1, C, 1, P, 1, P)
    bound = 2.0 / np.sqrt(IN_D)
    return {"X": bf(X.reshape(B, C, IMG, IMG)),
            "W": bf(np.random.uniform(-bound, bound, (HID, IN_D)) / s[None, :]),
            "b": bf(np.random.standard_normal(HID) * 0.3),
            "class_token": bf(np.random.uniform(0.0, 1.0, (1, HID))),
            "pos_embed": bf(positional_embedding(SEQ, HID))}


def reference(X, W, b, class_token, pos_embed):
    nb = X.shape[0]
    patches = f64(X).reshape(nb, C, NP, P, NP, P)
    patches = patches.transpose(0, 2, 4, 1, 3, 5).reshape(nb, NP * NP, IN_D)
    tokens = (mxq(patches, 2, "e4m3") @ mxq(f64(W), 1, "e4m3").T) + f64(b)
    cls = np.broadcast_to(f64(class_token)[None, :, :], (nb, 1, HID))
    tokens = np.concatenate([cls, tokens], axis=1)
    return tokens * f64(pos_embed)[None, :, :]

@@ -1,0 +1,249 @@
+from contextlib import ExitStack
+
+import concourse.mybir as mybir
+from concourse.masks import make_identity
+
+F32 = mybir.dt.float32
+BF16 = mybir.dt.bfloat16
+U32 = mybir.dt.uint32
+U8 = mybir.dt.uint8
+FP8X4 = mybir.dt.float8_e4m3fn_x4
+ADD = mybir.AluOpType.add
+MULT = mybir.AluOpType.mult
+
+P = 128
+HID = 512
+NG = 6
+NCHUNK = 12
+FLOPS = 2 * 2048 * 3072 * 512
+
+
+def tile_myvit_kernel(tc, X, W, b, class_token, pos_embed, out):
+    nc = tc.nc
+    with ExitStack() as ctx:
+        ctx.enter_context(tc.manual_schedule())
+        keep = ctx.enter_context(tc.tile_pool(name="keep", bufs=1))
+        rawp = ctx.enter_context(tc.tile_pool(name="rawp", bufs=5))
+        work = ctx.enter_context(tc.tile_pool(name="work", bufs=2))
+        outp = ctx.enter_context(tc.tile_pool(name="outp", bufs=4))
+        psum = ctx.enter_context(tc.psum_pool(name="psum", bufs=1))
+
+        ident = keep.tile([P, P], F32, name="ident")
+        make_identity(nc, ident[:])
+        bias = keep.tile([P, HID], BF16, name="bias")
+        nc.scalar.dma_start(out=bias[:], in_=b.partition_broadcast(P))
+        ct = keep.tile([32, HID], BF16, name="ct")
+        nc.scalar.dma_start(out=ct[:], in_=class_token.broadcast_to([32, HID]))
+        p0 = keep.tile([32, HID], BF16, name="p0")
+        nc.scalar.dma_start(out=p0[:], in_=pos_embed[0:1, :].broadcast_to([32, HID]))
+        cls = keep.tile([32, HID], F32, name="cls")
+        nc.gpsimd.tensor_tensor(out=cls[:], in0=ct[:], in1=p0[:], op=MULT)
+
+        wraw = [keep.tile([P, 4, 1024], BF16, name="wraw%d" % i) for i in range(3)]
+        w_view = W.rearrange("(t p) k -> p t k", p=P)
+        posq = [keep.tile([P, 8 * HID], BF16, name="posq%d" % qt) for qt in range(2)]
+        pos_view = pos_embed[1:65, :].rearrange("(t l g) h -> l t (g h)", t=2, l=4, g=8)
+
+        xc = [keep.tile([P, 1024], U32, name="xc%d" % s, align_bytes=64) for s in range(NCHUNK)]
+        xs = [keep.tile([P, 1024], U8, name="xs%d" % s, align_bytes=64) for s in range(NCHUNK)]
+        wc = [keep.tile([P, HID], U32, name="wc%d" % g, align_bytes=64) for g in range(NG)]
+        ws = [keep.tile([P, HID], U8, name="ws%d" % g, align_bytes=64) for g in range(NG)]
+
+        raws = {}
+        rgs = {}
+
+        def load_w(i):
+            nc.sync.dma_start(out=wraw[i][:], in_=w_view[:, :, i * 1024:(i + 1) * 1024])
+
+        def load_x(s):
+            qt, g = divmod(s, NG)
+            c, a = divmod(g, 2)
+            raw = rawp.tile([P, 4096], BF16, name="raw%d" % s, tag="raw")
+            for l in range(4):
+                y0 = (qt * 4 + l) * 32 + a * 16
+                nc.sync.dma_start(out=raw[l:P:4, :], in_=X[:, c, y0:y0 + 16, :].rearrange("b y x -> b (y x)"))
+            raws[s] = raw
+
+        def load_pos(qt):
+            for l in range(4):
+                nc.sync.dma_start(out=posq[qt][l:P:4, :], in_=pos_view[l, qt:qt + 1, :].broadcast_to([32, 8 * HID]))
+
+        def regroup(s):
+            nv = 16 if s < NG else 8
+            rg = work.tile([P, 4096], BF16, name="rg%d" % s, tag="rg")
+            nc.vector.tensor_copy(
+                out=rg[:].bitcast(F32).rearrange("p (g y w) -> p g y w", g=16, w=8)[:, 0:nv, :, :],
+                in_=raws[s][:].bitcast(F32).rearrange("p (y g w) -> p g y w", g=16, w=8)[:, 0:nv, :, :],
+            )
+            if nv < 16:
+                nc.scalar.copy(
+                    out=rg[:].bitcast(F32).rearrange("p (g y w) -> p g y w", g=16, w=8)[:, nv:16, :, :],
+                    in_=raws[s][:].bitcast(F32).rearrange("p (y g w) -> p g y w", g=16, w=8)[:, nv:16, :, :],
+                )
+            rgs[s] = rg
+
+        state = {"rot": 0, "n": 0, "e1": 0, "e2": 0}
+
+        def t_bank():
+            i = 4 + state["rot"]
+            state["rot"] = (state["rot"] + 1) % 4
+            state["n"] += 1
+            return psum.tile([P, 4, P], F32, name="tp%d" % state["n"], tag="bk%d" % i)
+
+        wgrs = {}
+        wrgs = {}
+
+        def regroup_w(i):
+            wrg = work.tile([P, 4096], BF16, name="wrg%d" % i, tag="wrg", bufs=1)
+            for u in range(2):
+                nc.vector.tensor_copy(
+                    out=wrg[:].bitcast(F32).rearrange("p (g u y w) -> p g u y w", g=8, u=2, w=8)[:, :, u, :, :],
+                    in_=wraw[i][:].rearrange("p t k -> p (t k)").bitcast(F32).rearrange("p (g y u w) -> p g y u w", g=8, u=2, w=8)[:, :, :, u, :],
+                )
+            wrgs[i] = wrg
+
+        def transpose_w(g):
+            wgr = work.tile([P, 2048], BF16, name="wgr%d" % g, tag="wgr", align_bytes=64)
+            wgrf = wgr[:].bitcast(F32).rearrange("p (t h u) -> p t h u", t=4, u=2)
+            for j in range(2):
+                bank = t_bank()
+                for tl in range(2):
+                    src = wrgs[g // 2][:].bitcast(F32)
+                    for u in range(2):
+                        k0 = (2 * j + tl) * 512 + (g % 2) * 256 + u * 128
+                        nc.tensor.transpose(out=bank[:, 2 * tl + u, :], in_=src[:, k0:k0 + 128], identity=ident[:])
+                nc.scalar.copy(out=wgrf[:, 2 * j:2 * j + 2, :, :], in_=bank[:].rearrange("p (t u) h -> p t h u", u=2))
+            wgrs[g] = wgr
+
+        grs = {}
+
+        def transpose_x(s, hf):
+            if hf == 0:
+                grs[s] = work.tile([P, 4096], BF16, name="gr%d" % s, tag="gr", align_bytes=64)
+            grf = grs[s][:].bitcast(F32).rearrange("p (g q u) -> p g q u", g=8, u=2)
+            rgf = rgs[s][:].bitcast(F32)
+            for j in range(2):
+                bank = t_bank()
+                g0 = 4 * hf + 2 * j
+                for gl in range(2):
+                    for u in range(2):
+                        k0 = (g0 + gl) * 256 + u * 128
+                        nc.tensor.transpose(out=bank[:, 2 * gl + u, :], in_=rgf[:, k0:k0 + 128], identity=ident[:])
+                nc.scalar.copy(out=grf[:, g0:g0 + 2, :, :], in_=bank[:].rearrange("p (g u) q -> p g q u", u=2))
+
+        def quant_w(g):
+            nc.vector.quantize_mx(out=wc[g][:].bitcast(FP8X4), scales=ws[g][:], in_=wgrs[g][:])
+
+        def quant_x(s, hf):
+            nc.vector.quantize_mx(
+                out=xc[s][:, hf * 512:(hf + 1) * 512].bitcast(FP8X4),
+                scales=xs[s][:, hf * 512:(hf + 1) * 512],
+                in_=grs[s][:, hf * 2048:(hf + 1) * 2048],
+            )
+
+        accs = {}
+        closed = []
+
+        def mx_pass(qt, gx, g, bank):
+            if g == 0:
+                accs[(qt, gx)] = psum.tile([P, HID], F32, name="acc%d_%d" % (qt, gx), tag="bk%d" % bank)
+            s = qt * NG + g
+            nc.tensor.matmul_mx(
+                out=accs[(qt, gx)][:],
+                lhsT=xc[s][:, gx * P:(gx + 1) * P].bitcast(FP8X4),
+                lhsT_scale=xs[s][:, gx * P:(gx + 1) * P],
+                rhs=wc[g][:].bitcast(FP8X4),
+                rhs_scale=ws[g][:],
+                start=(g == 0),
+                stop=(g == NG - 1),
+            )
+            if g == NG - 1:
+                closed.append((qt, gx))
+
+        osts = {}
+        tmps = {}
+
+        def add_bias():
+            for qt, gx in closed[state["e1"]:]:
+                tmp = outp.tile([P, HID], F32, name="tmp%d_%d" % (qt, gx), tag="tmp", bufs=6)
+                nc.vector.tensor_tensor(out=tmp[:], in0=accs[(qt, gx)][:], in1=bias[:], op=ADD)
+                tmps[(qt, gx)] = tmp
+            state["e1"] = len(closed)
+
+        def times_pos():
+            for qt, gx in closed[state["e2"]:]:
+                if gx % 2 == 0:
+                    osts[(qt, gx // 2)] = outp.tile([P, 2, HID], F32, name="ost%d_%d" % (qt, gx // 2), tag="ost")
+                ost = osts[(qt, gx // 2)]
+                on_pool = (qt == 0 and gx < 4) or (qt == 1 and gx % 2 == 0)
+                eng = nc.gpsimd if on_pool else nc.vector
+                eng.tensor_tensor(out=ost[:, gx % 2, :], in0=tmps[(qt, gx)][:], in1=posq[qt][:, gx * HID:(gx + 1) * HID], op=MULT)
+                if gx % 2 == 1:
+                    for l in range(4):
+                        r0 = 1 + (qt * 4 + l) * 8 + gx - 1
+                        nc.sync.dma_start(
+                            out=out[:, r0:r0 + 2, :].rearrange("b g h -> b (g h)"),
+                            in_=ost[l:P:4, :, :].rearrange("p g h -> p (g h)"),
+                        )
+            state["e2"] = len(closed)
+
+        def early(s):
+            qt, g = divmod(s, NG)
+            for gx in range(4):
+                mx_pass(qt, gx, g, gx)
+
+        def whole_group(qt, gx, bank):
+            for g in range(NG):
+                mx_pass(qt, gx, g, bank)
+
+        load_x(0)
+        load_w(0)
+        load_x(1)
+        load_x(2)
+        load_w(1)
+        load_x(3)
+        load_x(4)
+        load_w(2)
+        regroup(0)
+        regroup_w(0)
+
+        for t in range(NCHUNK):
+            if t < NG:
+                transpose_x(t, 0)
+                transpose_w(t)
+                if t >= 1:
+                    early(t - 1)
+                transpose_x(t, 1)
+            else:
+                first = 4 + state["rot"]
+                transpose_x(t, 0)
+                transpose_x(t, 1)
+                if t < NG + 4:
+                    whole_group(0, t - 2, first)
+                    state["rot"] = (state["rot"] + 1) % 4
+                early(t - 1)
+            if t + 1 < NCHUNK:
+                regroup(t + 1)
+            if t in (1, 3):
+                regroup_w((t + 1) // 2)
+            if t + 5 < NCHUNK:
+                load_x(t + 5)
+            if t == 2:
+                load_pos(0)
+            if t == 6:
+                load_pos(1)
+            if t < NG:
+                quant_w(t)
+            quant_x(t, 0)
+            quant_x(t, 1)
+            add_bias()
+            times_pos()
+
+        nc.sync.dma_start(out=out[:, 0, :], in_=cls[:])
+        early(NCHUNK - 1)
+        add_bias()
+        times_pos()
+        for i in range(4):
+            whole_group(1, 4 + i, 4 + (state["rot"] + i) % 4)
+            add_bias()
+            times_pos()

@@ -13,9 +13,37 @@ MULT = mybir.AluOpType.mult
 
 P = 128
 HID = 512
-NG = 6
 NCHUNK = 12
+OCT = 16
+SLOTW = 128
+WIN = (0, 12, 30, 48)
 FLOPS = 2 * 2048 * 3072 * 512
+
+
+def place(j):
+    pair, r = divmod(j, 6)
+    e, c = divmod(r, 3)
+    return 6 * pair + 2 * c + e
+
+
+def order_of(i):
+    return sorted(range(OCT), key=lambda j: place(OCT * i + j))
+
+
+def runs_of(i):
+    places = [place(OCT * i + j) for j in order_of(i)]
+    out = []
+    for n, s in enumerate(places):
+        nxt = s >= WIN[i + 1]
+        rel = s - (WIN[i + 1] if nxt else WIN[i])
+        if out and out[-1][1] == nxt:
+            q0, x, first, count, step = out[-1]
+            d = rel - (first + (count - 1) * step)
+            if count == 1 or d == step:
+                out[-1] = (q0, x, first, count + 1, d)
+                continue
+        out.append((8 * n, nxt, rel, 1, 1))
+    return out
 
 
 def tile_myvit_kernel(tc, X, W, b, class_token, pos_embed, out):
@@ -23,227 +51,245 @@ def tile_myvit_kernel(tc, X, W, b, class_token, pos_embed, out):
     with ExitStack() as ctx:
         ctx.enter_context(tc.manual_schedule())
         keep = ctx.enter_context(tc.tile_pool(name="keep", bufs=1))
-        rawp = ctx.enter_context(tc.tile_pool(name="rawp", bufs=5))
+        rawp = ctx.enter_context(tc.tile_pool(name="rawp", bufs=6))
         work = ctx.enter_context(tc.tile_pool(name="work", bufs=2))
+        codes = ctx.enter_context(tc.tile_pool(name="codes", bufs=4))
         outp = ctx.enter_context(tc.tile_pool(name="outp", bufs=4))
         psum = ctx.enter_context(tc.psum_pool(name="psum", bufs=1))
+
+        raws, wraws = {}, {}
+        x_rows = X.rearrange("b c (g a y) x -> (b c g) a (y x)", g=8, a=2)
+        w_view = W.rearrange("(t p) (c a k) -> c a p t k", p=P, c=3, a=2)
+
+        def load_x(t):
+            m, a = divmod(t, 2)
+            raw = rawp.tile([P, 4096], BF16, name="raw%d" % t, tag="raw")
+            nc.sync.dma_start(out=raw[:], in_=x_rows[m * P:(m + 1) * P, a, :])
+            raws[t] = raw
+
+        def load_w(c, a):
+            wr = keep.tile([P, 4, 512], BF16, name="wraw%d%d" % (c, a))
+            nc.sync.dma_start(out=wr[:], in_=w_view[c, a])
+            wraws[(c, a)] = wr
+
+        load_x(0)
+        load_x(1)
+        for a in range(2):
+            for c in range(3):
+                load_w(c, a)
+        for t in range(2, 6):
+            load_x(t)
 
         ident = keep.tile([P, P], F32, name="ident")
         make_identity(nc, ident[:])
         bias = keep.tile([P, HID], BF16, name="bias")
         nc.scalar.dma_start(out=bias[:], in_=b.partition_broadcast(P))
+        pos = keep.tile([P, HID], BF16, name="pos")
+        for e in range(2):
+            nc.scalar.dma_start(out=pos[64 * e:64 * e + 64, :], in_=pos_embed[1:65, :])
         ct = keep.tile([32, HID], BF16, name="ct")
         nc.scalar.dma_start(out=ct[:], in_=class_token.broadcast_to([32, HID]))
         p0 = keep.tile([32, HID], BF16, name="p0")
         nc.scalar.dma_start(out=p0[:], in_=pos_embed[0:1, :].broadcast_to([32, HID]))
         cls = keep.tile([32, HID], F32, name="cls")
+
+        perm = []
+        for i in range(3):
+            pm = keep.tile([P, P], F32, name="perm%d" % i)
+            eng = nc.vector if i == 0 else nc.gpsimd
+            for n, j in enumerate(order_of(i)):
+                eng.tensor_copy(out=pm[:, 8 * n:8 * n + 8], in_=ident[:, 8 * j:8 * j + 8])
+            perm.append(pm)
         nc.gpsimd.tensor_tensor(out=cls[:], in0=ct[:], in1=p0[:], op=MULT)
 
-        wraw = [keep.tile([P, 4, 1024], BF16, name="wraw%d" % i) for i in range(3)]
-        w_view = W.rearrange("(t p) k -> p t k", p=P)
-        posq = [keep.tile([P, 8 * HID], BF16, name="posq%d" % qt) for qt in range(2)]
-        pos_view = pos_embed[1:65, :].rearrange("(t l g) h -> l t (g h)", t=2, l=4, g=8)
+        wc = {}
+        ws = {}
+        for a in range(2):
+            for c in range(3):
+                wcode = keep.tile([P, HID], U32, name="wc%d%d" % (c, a), align_bytes=64)
+                wscale = keep.tile([P, HID], U8, name="ws%d%d" % (c, a), align_bytes=64)
+                wc[(c, a)], ws[(c, a)] = wcode, wscale
 
-        xc = [keep.tile([P, 1024], U32, name="xc%d" % s, align_bytes=64) for s in range(NCHUNK)]
-        xs = [keep.tile([P, 1024], U8, name="xs%d" % s, align_bytes=64) for s in range(NCHUNK)]
-        wc = [keep.tile([P, HID], U32, name="wc%d" % g, align_bytes=64) for g in range(NG)]
-        ws = [keep.tile([P, HID], U8, name="ws%d" % g, align_bytes=64) for g in range(NG)]
-
-        raws = {}
-        rgs = {}
-
-        def load_w(i):
-            nc.sync.dma_start(out=wraw[i][:], in_=w_view[:, :, i * 1024:(i + 1) * 1024])
-
-        def load_x(s):
-            qt, g = divmod(s, NG)
-            c, a = divmod(g, 2)
-            raw = rawp.tile([P, 4096], BF16, name="raw%d" % s, tag="raw")
-            for l in range(4):
-                y0 = (qt * 4 + l) * 32 + a * 16
-                nc.sync.dma_start(out=raw[l:P:4, :], in_=X[:, c, y0:y0 + 16, :].rearrange("b y x -> b (y x)"))
-            raws[s] = raw
-
-        def load_pos(qt):
-            for l in range(4):
-                nc.sync.dma_start(out=posq[qt][l:P:4, :], in_=pos_view[l, qt:qt + 1, :].broadcast_to([32, 8 * HID]))
-
-        def regroup(s):
-            nv = 16 if s < NG else 8
-            rg = work.tile([P, 4096], BF16, name="rg%d" % s, tag="rg")
-            nc.vector.tensor_copy(
-                out=rg[:].bitcast(F32).rearrange("p (g y w) -> p g y w", g=16, w=8)[:, 0:nv, :, :],
-                in_=raws[s][:].bitcast(F32).rearrange("p (y g w) -> p g y w", g=16, w=8)[:, 0:nv, :, :],
-            )
-            if nv < 16:
-                nc.scalar.copy(
-                    out=rg[:].bitcast(F32).rearrange("p (g y w) -> p g y w", g=16, w=8)[:, nv:16, :, :],
-                    in_=raws[s][:].bitcast(F32).rearrange("p (y g w) -> p g y w", g=16, w=8)[:, nv:16, :, :],
-                )
-            rgs[s] = rg
-
-        state = {"rot": 0, "n": 0, "e1": 0, "e2": 0}
+        rgs, wrgs, grs, wgrs, xcs, xss = {}, {}, {}, {}, {}, {}
+        state = {"rot": 0, "n": 0}
 
         def t_bank():
-            i = 4 + state["rot"]
-            state["rot"] = (state["rot"] + 1) % 4
+            k = 3 + state["rot"]
+            state["rot"] = (state["rot"] + 1) % 5
             state["n"] += 1
-            return psum.tile([P, 4, P], F32, name="tp%d" % state["n"], tag="bk%d" % i)
+            return psum.tile([P, 4, P], F32, name="tp%d" % state["n"], tag="bk%d" % k)
 
-        wgrs = {}
-        wrgs = {}
+        def regroup(t, nv):
+            rg = work.tile([P, 4096], BF16, name="rg%d" % t, tag="rg")
+            o = rg[:].bitcast(F32).rearrange("p (g y w) -> p g y w", g=16, w=8)
+            i = raws[t][:].bitcast(F32).rearrange("p (y g w) -> p g y w", g=16, w=8)
+            nc.vector.tensor_copy(out=o[:, 0:nv, :, :], in_=i[:, 0:nv, :, :])
+            rgs[t] = (rg, o, i, nv)
 
-        def regroup_w(i):
-            wrg = work.tile([P, 4096], BF16, name="wrg%d" % i, tag="wrg", bufs=1)
+        def regroup_rest(t):
+            rg, o, i, nv = rgs[t]
+            if nv < 16:
+                nc.scalar.copy(out=o[:, nv:16, :, :], in_=i[:, nv:16, :, :])
+
+        def regroup_w(c, a):
+            wrg = work.tile([P, 2048], BF16, name="wrg%d%d" % (c, a), tag="wrg")
             for u in range(2):
                 nc.vector.tensor_copy(
-                    out=wrg[:].bitcast(F32).rearrange("p (g u y w) -> p g u y w", g=8, u=2, w=8)[:, :, u, :, :],
-                    in_=wraw[i][:].rearrange("p t k -> p (t k)").bitcast(F32).rearrange("p (g y u w) -> p g y u w", g=8, u=2, w=8)[:, :, :, u, :],
+                    out=wrg[:].bitcast(F32).rearrange("p (t u y w) -> p t u y w", t=4, u=2, w=8)[:, :, u, :, :],
+                    in_=wraws[(c, a)][:].rearrange("p t k -> p (t k)").bitcast(F32).rearrange("p (t y u w) -> p t y u w", t=4, u=2, w=8)[:, :, :, u, :],
                 )
-            wrgs[i] = wrg
+            wrgs[(c, a)] = wrg
 
-        def transpose_w(g):
-            wgr = work.tile([P, 2048], BF16, name="wgr%d" % g, tag="wgr", align_bytes=64)
+        def gr_tile(t):
+            if t not in grs and t < NCHUNK:
+                gr = work.tile([P, 18 * 2 * SLOTW], BF16, name="gr%d" % t, tag="gr%d" % (t % 2), align_bytes=64)
+                grs[t] = gr
+
+        def transpose_x(t, vector_banks=()):
+            i = (t // 2) % 3
+            gr_tile(t)
+            if i < 2:
+                gr_tile(t + 2)
+            rgf = rgs[t][0][:].bitcast(F32)
+            for j in range(4):
+                bank = t_bank()
+                for v in range(4):
+                    k0 = (4 * j + v) * P
+                    nc.tensor.transpose(out=bank[:, v, :], in_=rgf[:, k0:k0 + P], identity=perm[i][:])
+                for q0, nxt, first, count, step in runs_of(i):
+                    gr = grs[t + 2 if nxt else t]
+                    dst = gr[:].bitcast(F32).rearrange("p (s q w) -> p s q w", q=8, w=16)
+                    dst = dst[:, first:first + (count - 1) * step + 1:step, :, 4 * j:4 * j + 4]
+                    src = bank[:, :, q0:q0 + 8 * count].rearrange("p v (s q) -> p s q v", q=8)
+                    if j in vector_banks:
+                        nc.vector.tensor_copy(out=dst, in_=src)
+                    else:
+                        nc.scalar.copy(out=dst, in_=src)
+
+        def transpose_w(c, a, vector_banks):
+            wgr = work.tile([P, 2048], BF16, name="wgr%d%d" % (c, a), tag="wgr", align_bytes=64)
             wgrf = wgr[:].bitcast(F32).rearrange("p (t h u) -> p t h u", t=4, u=2)
+            src = wrgs[(c, a)][:].bitcast(F32)
             for j in range(2):
                 bank = t_bank()
-                for tl in range(2):
-                    src = wrgs[g // 2][:].bitcast(F32)
-                    for u in range(2):
-                        k0 = (2 * j + tl) * 512 + (g % 2) * 256 + u * 128
-                        nc.tensor.transpose(out=bank[:, 2 * tl + u, :], in_=src[:, k0:k0 + 128], identity=ident[:])
-                nc.scalar.copy(out=wgrf[:, 2 * j:2 * j + 2, :, :], in_=bank[:].rearrange("p (t u) h -> p t h u", u=2))
-            wgrs[g] = wgr
+                for v in range(4):
+                    k0 = (4 * j + v) * P
+                    nc.tensor.transpose(out=bank[:, v, :], in_=src[:, k0:k0 + P], identity=ident[:])
+                copy = nc.vector.tensor_copy if j in vector_banks else nc.scalar.copy
+                copy(out=wgrf[:, 2 * j:2 * j + 2, :, :], in_=bank[:].rearrange("p (t u) h -> p t h u", u=2))
+            wgrs[(c, a)] = wgr
 
-        grs = {}
+        def quant_w(c, a):
+            nc.vector.quantize_mx(out=wc[(c, a)][:].bitcast(FP8X4), scales=ws[(c, a)][:], in_=wgrs[(c, a)][:])
 
-        def transpose_x(s, hf):
-            if hf == 0:
-                grs[s] = work.tile([P, 4096], BF16, name="gr%d" % s, tag="gr", align_bytes=64)
-            grf = grs[s][:].bitcast(F32).rearrange("p (g q u) -> p g q u", g=8, u=2)
-            rgf = rgs[s][:].bitcast(F32)
-            for j in range(2):
-                bank = t_bank()
-                g0 = 4 * hf + 2 * j
-                for gl in range(2):
-                    for u in range(2):
-                        k0 = (g0 + gl) * 256 + u * 128
-                        nc.tensor.transpose(out=bank[:, 2 * gl + u, :], in_=rgf[:, k0:k0 + 128], identity=ident[:])
-                nc.scalar.copy(out=grf[:, g0:g0 + 2, :, :], in_=bank[:].rearrange("p (g u) q -> p g q u", u=2))
-
-        def quant_w(g):
-            nc.vector.quantize_mx(out=wc[g][:].bitcast(FP8X4), scales=ws[g][:], in_=wgrs[g][:])
-
-        def quant_x(s, hf):
-            nc.vector.quantize_mx(
-                out=xc[s][:, hf * 512:(hf + 1) * 512].bitcast(FP8X4),
-                scales=xs[s][:, hf * 512:(hf + 1) * 512],
-                in_=grs[s][:, hf * 2048:(hf + 1) * 2048],
-            )
+        def quant_x(t):
+            i = (t // 2) % 3
+            n = WIN[i + 1] - WIN[i]
+            xc = codes.tile([P, 18 * 64], U32, name="xc%d" % t, tag="xc", align_bytes=64)
+            xs = codes.tile([P, 18 * 64], U8, name="xs%d" % t, tag="xs", align_bytes=64)
+            xcs[t], xss[t] = xc, xs
+            s = 0
+            while s < n:
+                k = 8
+                while s + k > n:
+                    k //= 2
+                if t < NCHUNK - 1 and s + 16 <= n:
+                    k = 16
+                nc.vector.quantize_mx(
+                    out=xc[:, s * 64:(s + k) * 64].bitcast(FP8X4),
+                    scales=xs[:, s * 64:(s + k) * 64],
+                    in_=grs[t][:, s * 256:(s + k) * 256],
+                )
+                s += k
 
         accs = {}
-        closed = []
+        to_add, to_mul = [], []
 
-        def mx_pass(qt, gx, g, bank):
-            if g == 0:
-                accs[(qt, gx)] = psum.tile([P, HID], F32, name="acc%d_%d" % (qt, gx), tag="bk%d" % bank)
-            s = qt * NG + g
-            nc.tensor.matmul_mx(
-                out=accs[(qt, gx)][:],
-                lhsT=xc[s][:, gx * P:(gx + 1) * P].bitcast(FP8X4),
-                lhsT_scale=xs[s][:, gx * P:(gx + 1) * P],
-                rhs=wc[g][:].bitcast(FP8X4),
-                rhs_scale=ws[g][:],
-                start=(g == 0),
-                stop=(g == NG - 1),
-            )
-            if g == NG - 1:
-                closed.append((qt, gx))
+        def mx_passes(t):
+            m, a = divmod(t, 2)
+            i = m % 3
+            for k, pair in enumerate(range(WIN[i] // 6, WIN[i + 1] // 6)):
+                if a == 0:
+                    acc = psum.tile([P, HID], F32, name="acc%d_%d" % (m, pair), tag="bk%d" % k)
+                    accs[(m, pair)] = acc
+                acc = accs[(m, pair)]
+                for c in range(3):
+                    s0 = (6 * pair + 2 * c - WIN[i]) * 64
+                    nc.tensor.matmul_mx(
+                        out=acc[:],
+                        lhsT=xcs[t][:, s0:s0 + P].bitcast(FP8X4),
+                        lhsT_scale=xss[t][:, s0:s0 + P],
+                        rhs=wc[(c, a)][:].bitcast(FP8X4),
+                        rhs_scale=ws[(c, a)][:],
+                        start=(a == 0 and c == 0),
+                        stop=(a == 1 and c == 2),
+                    )
+                if a == 1:
+                    to_add.append((acc, 16 * (m // 3) + 2 * pair))
 
-        osts = {}
-        tmps = {}
+        def add_bias(n):
+            for acc, b0 in to_add[:n]:
+                tmp = outp.tile([P, HID], F32, name="tmp%d" % b0, tag="tmp")
+                nc.vector.tensor_tensor(out=tmp[:], in0=acc[:], in1=bias[:], op=ADD)
+                to_mul.append((tmp, b0))
+            to_add[:n] = []
 
-        def add_bias():
-            for qt, gx in closed[state["e1"]:]:
-                tmp = outp.tile([P, HID], F32, name="tmp%d_%d" % (qt, gx), tag="tmp", bufs=6)
-                nc.vector.tensor_tensor(out=tmp[:], in0=accs[(qt, gx)][:], in1=bias[:], op=ADD)
-                tmps[(qt, gx)] = tmp
-            state["e1"] = len(closed)
+        def times_pos(n):
+            for tmp, b0 in to_mul[:n]:
+                ost = outp.tile([P, HID], F32, name="ost%d" % b0, tag="ost")
+                nc.vector.tensor_tensor(out=ost[:], in0=tmp[:], in1=pos[:], op=MULT)
+                for e in range(2):
+                    nc.sync.dma_start(out=out[b0 + e, 1:65, :], in_=ost[64 * e:64 * e + 64, :])
+            to_mul[:n] = []
 
-        def times_pos():
-            for qt, gx in closed[state["e2"]:]:
-                if gx % 2 == 0:
-                    osts[(qt, gx // 2)] = outp.tile([P, 2, HID], F32, name="ost%d_%d" % (qt, gx // 2), tag="ost")
-                ost = osts[(qt, gx // 2)]
-                on_pool = (qt == 0 and gx < 4) or (qt == 1 and gx % 2 == 0)
-                eng = nc.gpsimd if on_pool else nc.vector
-                eng.tensor_tensor(out=ost[:, gx % 2, :], in0=tmps[(qt, gx)][:], in1=posq[qt][:, gx * HID:(gx + 1) * HID], op=MULT)
-                if gx % 2 == 1:
-                    for l in range(4):
-                        r0 = 1 + (qt * 4 + l) * 8 + gx - 1
-                        nc.sync.dma_start(
-                            out=out[:, r0:r0 + 2, :].rearrange("b g h -> b (g h)"),
-                            in_=ost[l:P:4, :, :].rearrange("p g h -> p (g h)"),
-                        )
-            state["e2"] = len(closed)
-
-        def early(s):
-            qt, g = divmod(s, NG)
-            for gx in range(4):
-                mx_pass(qt, gx, g, gx)
-
-        def whole_group(qt, gx, bank):
-            for g in range(NG):
-                mx_pass(qt, gx, g, bank)
-
-        load_x(0)
-        load_w(0)
-        load_x(1)
-        load_x(2)
-        load_w(1)
-        load_x(3)
-        load_x(4)
-        load_w(2)
-        regroup(0)
-        regroup_w(0)
-
-        for t in range(NCHUNK):
-            if t < NG:
-                transpose_x(t, 0)
-                transpose_w(t)
-                if t >= 1:
-                    early(t - 1)
-                transpose_x(t, 1)
-            else:
-                first = 4 + state["rot"]
-                transpose_x(t, 0)
-                transpose_x(t, 1)
-                if t < NG + 4:
-                    whole_group(0, t - 2, first)
-                    state["rot"] = (state["rot"] + 1) % 4
-                early(t - 1)
-            if t + 1 < NCHUNK:
-                regroup(t + 1)
-            if t in (1, 3):
-                regroup_w((t + 1) // 2)
-            if t + 5 < NCHUNK:
-                load_x(t + 5)
-            if t == 2:
-                load_pos(0)
-            if t == 6:
-                load_pos(1)
-            if t < NG:
-                quant_w(t)
-            quant_x(t, 0)
-            quant_x(t, 1)
-            add_bias()
-            times_pos()
-
+        regroup(0, 16)
+        transpose_x(0)
+        regroup(1, 16)
+        load_x(6)
+        transpose_x(1)
+        load_x(7)
+        regroup_w(0, 0)
+        transpose_w(0, 0, (1,))
+        quant_x(0)
+        regroup_w(1, 0)
+        transpose_w(1, 0, ())
+        regroup_w(2, 0)
+        quant_w(0, 0)
+        transpose_w(2, 0, (1,))
+        quant_x(1)
+        quant_w(1, 0)
+        regroup_w(0, 1)
+        transpose_w(0, 1, ())
+        quant_w(2, 0)
+        regroup_w(1, 1)
+        transpose_w(1, 1, (1,))
+        mx_passes(0)
+        regroup_w(2, 1)
+        quant_w(0, 1)
+        transpose_w(2, 1, (1,))
+        quant_w(1, 1)
+        regroup(2, 10)
+        quant_w(2, 1)
         nc.sync.dma_start(out=out[:, 0, :], in_=cls[:])
-        early(NCHUNK - 1)
-        add_bias()
-        times_pos()
-        for i in range(4):
-            whole_group(1, 4 + i, 4 + (state["rot"] + i) % 4)
-            add_bias()
-            times_pos()
+        regroup_rest(2)
+        for t in range(2, NCHUNK):
+            if t % 2 == 1:
+                add_bias(2)
+            if t + 1 < NCHUNK:
+                regroup(t + 1, 10)
+            if t + 6 < NCHUNK:
+                load_x(t + 6)
+            transpose_x(t, (1, 3) if t == NCHUNK - 1 else ())
+            times_pos(1)
+            mx_passes(t - 1)
+            if t % 2 == 0:
+                times_pos(2)
+                add_bias(1)
+            if t + 1 < NCHUNK:
+                regroup_rest(t + 1)
+            quant_x(t)
+        mx_passes(NCHUNK - 1)
+        times_pos(3)
+        for n in range(3):
+            add_bias(1)
+            times_pos(1)

@@ -72,25 +72,29 @@ def tile_myvit_kernel(tc, X, W, b, class_token, pos_embed, out):
             nc.sync.dma_start(out=wr[:], in_=w_view[c, a])
             wraws[(c, a)] = wr
 
+        SEQ = [0, 2, 1] + list(range(3, NCHUNK))
         load_x(0)
+        for c in range(3):
+            load_w(c, 0)
+        load_x(2)
         load_x(1)
-        for a in range(2):
-            for c in range(3):
-                load_w(c, a)
-        for t in range(2, 6):
+        for c in range(3):
+            load_w(c, 1)
+        bias = keep.tile([P, HID], BF16, name="bias")
+        nc.sync.dma_start(out=bias[:], in_=b.partition_broadcast(P))
+        pos = keep.tile([P, HID], BF16, name="pos")
+        for e in range(2):
+            nc.sync.dma_start(out=pos[64 * e:64 * e + 64, :], in_=pos_embed[1:65, :])
+        ct = keep.tile([32, HID], BF16, name="ct")
+        nc.sync.dma_start(out=ct[:], in_=class_token.broadcast_to([32, HID]))
+        p0 = keep.tile([32, HID], BF16, name="p0")
+        nc.sync.dma_start(out=p0[:], in_=pos_embed[0:1, :].broadcast_to([32, HID]))
+
+        for t in range(3, 6):
             load_x(t)
 
         ident = keep.tile([P, P], F32, name="ident")
         make_identity(nc, ident[:])
-        bias = keep.tile([P, HID], BF16, name="bias")
-        nc.scalar.dma_start(out=bias[:], in_=b.partition_broadcast(P))
-        pos = keep.tile([P, HID], BF16, name="pos")
-        for e in range(2):
-            nc.scalar.dma_start(out=pos[64 * e:64 * e + 64, :], in_=pos_embed[1:65, :])
-        ct = keep.tile([32, HID], BF16, name="ct")
-        nc.scalar.dma_start(out=ct[:], in_=class_token.broadcast_to([32, HID]))
-        p0 = keep.tile([32, HID], BF16, name="p0")
-        nc.scalar.dma_start(out=p0[:], in_=pos_embed[0:1, :].broadcast_to([32, HID]))
         cls = keep.tile([32, HID], F32, name="cls")
 
         perm = []
@@ -111,13 +115,14 @@ def tile_myvit_kernel(tc, X, W, b, class_token, pos_embed, out):
                 wc[(c, a)], ws[(c, a)] = wcode, wscale
 
         rgs, wrgs, grs, wgrs, xcs, xss = {}, {}, {}, {}, {}, {}
-        state = {"rot": 0, "n": 0}
+        free = list(range(8))
+        count = {"t": 0}
 
         def t_bank():
-            k = 3 + state["rot"]
-            state["rot"] = (state["rot"] + 1) % 5
-            state["n"] += 1
-            return psum.tile([P, 4, P], F32, name="tp%d" % state["n"], tag="bk%d" % k)
+            k = free.pop(0)
+            free.append(k)
+            count["t"] += 1
+            return psum.tile([P, 4, P], F32, name="tp%d" % count["t"], tag="bk%d" % k)
 
         def regroup(t, nv):
             rg = work.tile([P, 4096], BF16, name="rg%d" % t, tag="rg")
@@ -132,7 +137,7 @@ def tile_myvit_kernel(tc, X, W, b, class_token, pos_embed, out):
                 nc.scalar.copy(out=o[:, nv:16, :, :], in_=i[:, nv:16, :, :])
 
         def regroup_w(c, a):
-            wrg = work.tile([P, 2048], BF16, name="wrg%d%d" % (c, a), tag="wrg")
+            wrg = work.tile([P, 2048], BF16, name="wrg%d%d" % (c, a), tag="wrg", bufs=3)
             for u in range(2):
                 nc.vector.tensor_copy(
                     out=wrg[:].bitcast(F32).rearrange("p (t u y w) -> p t u y w", t=4, u=2, w=8)[:, :, u, :, :],
@@ -142,7 +147,7 @@ def tile_myvit_kernel(tc, X, W, b, class_token, pos_embed, out):
 
         def gr_tile(t):
             if t not in grs and t < NCHUNK:
-                gr = work.tile([P, 18 * 2 * SLOTW], BF16, name="gr%d" % t, tag="gr%d" % (t % 2), align_bytes=64)
+                gr = work.tile([P, 18 * 2 * SLOTW], BF16, name="gr%d" % t, tag="gr%d" % (t % 2), bufs=3, align_bytes=64)
                 grs[t] = gr
 
         def transpose_x(t, vector_banks=()):
@@ -167,7 +172,7 @@ def tile_myvit_kernel(tc, X, W, b, class_token, pos_embed, out):
                         nc.scalar.copy(out=dst, in_=src)
 
         def transpose_w(c, a, vector_banks):
-            wgr = work.tile([P, 2048], BF16, name="wgr%d%d" % (c, a), tag="wgr", align_bytes=64)
+            wgr = work.tile([P, 2048], BF16, name="wgr%d%d" % (c, a), tag="wgr", bufs=3, align_bytes=64)
             wgrf = wgr[:].bitcast(F32).rearrange("p (t h u) -> p t h u", t=4, u=2)
             src = wrgs[(c, a)][:].bitcast(F32)
             for j in range(2):
@@ -208,11 +213,12 @@ def tile_myvit_kernel(tc, X, W, b, class_token, pos_embed, out):
         def mx_passes(t):
             m, a = divmod(t, 2)
             i = m % 3
-            for k, pair in enumerate(range(WIN[i] // 6, WIN[i + 1] // 6)):
+            for pair in range(WIN[i] // 6, WIN[i + 1] // 6):
                 if a == 0:
+                    k = free.pop(0)
                     acc = psum.tile([P, HID], F32, name="acc%d_%d" % (m, pair), tag="bk%d" % k)
-                    accs[(m, pair)] = acc
-                acc = accs[(m, pair)]
+                    accs[(m, pair)] = (acc, k)
+                acc, k = accs[(m, pair)]
                 for c in range(3):
                     s0 = (6 * pair + 2 * c - WIN[i]) * 64
                     nc.tensor.matmul_mx(
@@ -225,71 +231,79 @@ def tile_myvit_kernel(tc, X, W, b, class_token, pos_embed, out):
                         stop=(a == 1 and c == 2),
                     )
                 if a == 1:
-                    to_add.append((acc, 16 * (m // 3) + 2 * pair))
+                    to_add.append((acc, k, 16 * (m // 3) + 2 * pair))
 
         def add_bias(n):
-            for acc, b0 in to_add[:n]:
+            for acc, k, b0 in to_add[:n]:
+                free.append(k)
                 tmp = outp.tile([P, HID], F32, name="tmp%d" % b0, tag="tmp")
                 nc.vector.tensor_tensor(out=tmp[:], in0=acc[:], in1=bias[:], op=ADD)
                 to_mul.append((tmp, b0))
             to_add[:n] = []
 
-        def times_pos(n):
+        def times_pos(n, eng=nc.vector):
             for tmp, b0 in to_mul[:n]:
                 ost = outp.tile([P, HID], F32, name="ost%d" % b0, tag="ost")
-                nc.vector.tensor_tensor(out=ost[:], in0=tmp[:], in1=pos[:], op=MULT)
+                eng.tensor_tensor(out=ost[:], in0=tmp[:], in1=pos[:], op=MULT)
                 for e in range(2):
                     nc.sync.dma_start(out=out[b0 + e, 1:65, :], in_=ost[64 * e:64 * e + 64, :])
             to_mul[:n] = []
 
-        regroup(0, 16)
-        transpose_x(0)
-        regroup(1, 16)
-        load_x(6)
-        transpose_x(1)
-        load_x(7)
+        regroup(0, 10)
+        regroup_rest(0)
         regroup_w(0, 0)
-        transpose_w(0, 0, (1,))
-        quant_x(0)
+        transpose_x(0, (2,))
         regroup_w(1, 0)
-        transpose_w(1, 0, ())
         regroup_w(2, 0)
-        quant_w(0, 0)
-        transpose_w(2, 0, (1,))
-        quant_x(1)
-        quant_w(1, 0)
-        regroup_w(0, 1)
-        transpose_w(0, 1, ())
-        quant_w(2, 0)
-        regroup_w(1, 1)
-        transpose_w(1, 1, (1,))
-        mx_passes(0)
-        regroup_w(2, 1)
-        quant_w(0, 1)
-        transpose_w(2, 1, (1,))
-        quant_w(1, 1)
+        transpose_w(0, 0, ())
         regroup(2, 10)
-        quant_w(2, 1)
-        nc.sync.dma_start(out=out[:, 0, :], in_=cls[:])
+        quant_x(0)
+        transpose_w(1, 0, (1,))
         regroup_rest(2)
-        for t in range(2, NCHUNK):
-            if t % 2 == 1:
-                add_bias(2)
-            if t + 1 < NCHUNK:
-                regroup(t + 1, 10)
+        quant_w(0, 0)
+        transpose_w(2, 0, ())
+        regroup(1, 10)
+        quant_w(1, 0)
+        quant_w(2, 0)
+        load_x(6)
+        for k in range(1, NCHUNK):
+            t = SEQ[k]
+            nxt = SEQ[k + 1] if k + 1 < NCHUNK else None
+            started = len(to_add)
+            add_bias(started)
+            if nxt is not None and k > 1:
+                regroup(nxt, 10)
             if t + 6 < NCHUNK:
                 load_x(t + 6)
-            transpose_x(t, (1, 3) if t == NCHUNK - 1 else ())
-            times_pos(1)
-            mx_passes(t - 1)
-            if t % 2 == 0:
+            transpose_x(t, (1, 3) if k == NCHUNK - 1 else ())
+            if k == 1:
+                regroup_rest(1)
+                regroup_w(0, 1)
+            if k == 2:
+                regroup_w(1, 1)
+                transpose_w(0, 1, ())
+                regroup_w(2, 1)
+            if nxt is not None:
+                times_pos(1)
+            mx_passes(SEQ[k - 1])
+            if k == 2:
+                transpose_w(1, 1, (1,))
+                quant_w(0, 1)
+                transpose_w(2, 1, (1,))
+                quant_w(1, 1)
+            if started == 0:
                 times_pos(2)
-                add_bias(1)
-            if t + 1 < NCHUNK:
-                regroup_rest(t + 1)
-            quant_x(t)
-        mx_passes(NCHUNK - 1)
-        times_pos(3)
-        for n in range(3):
             add_bias(1)
-            times_pos(1)
+            if nxt is not None and k > 1:
+                regroup_rest(nxt)
+            quant_x(t)
+            if k == 2:
+                quant_w(2, 1)
+                nc.sync.dma_start(out=out[:, 0, :], in_=cls[:])
+        times_pos(2)
+        mx_passes(SEQ[-1])
+        times_pos(1, nc.gpsimd)
+        add_bias(1)
+        times_pos(1, nc.gpsimd)
+        add_bias(2)
+        times_pos(2)

@@ -57,6 +57,16 @@ def tile_myvit_kernel(tc, X, W, b, class_token, pos_embed, out):
         outp = ctx.enter_context(tc.tile_pool(name="outp", bufs=4))
         psum = ctx.enter_context(tc.psum_pool(name="psum", bufs=1))
 
+        ones = keep.tile([P, P], BF16, name="ones")
+        nc.gpsimd.memset(ones[:], 1.0)
+        rows = []
+        for r, src in enumerate((b.rearrange("(o h) -> o h", o=1), class_token, pos_embed[0:1, :])):
+            row = keep.tile([P, HID], BF16, name="row%d" % r)
+            nc.gpsimd.memset(row[:], 0.0)
+            nc.scalar.dma_start(out=row[0:1, :], in_=src)
+            rows.append(row)
+        pos = keep.tile([P, HID], BF16, name="pos")
+
         raws, wraws = {}, {}
         x_rows = X.rearrange("b c (g a y) x -> (b c g) a (y x)", g=8, a=2)
         w_view = W.rearrange("(t p) (c a k) -> c a p t k", p=P, c=3, a=2)
@@ -80,31 +90,20 @@ def tile_myvit_kernel(tc, X, W, b, class_token, pos_embed, out):
         load_x(1)
         for c in range(3):
             load_w(c, 1)
-        bias = keep.tile([P, HID], BF16, name="bias")
-        nc.sync.dma_start(out=bias[:], in_=b.partition_broadcast(P))
-        pos = keep.tile([P, HID], BF16, name="pos")
         for e in range(2):
             nc.sync.dma_start(out=pos[64 * e:64 * e + 64, :], in_=pos_embed[1:65, :])
-        ct = keep.tile([32, HID], BF16, name="ct")
-        nc.sync.dma_start(out=ct[:], in_=class_token.broadcast_to([32, HID]))
-        p0 = keep.tile([32, HID], BF16, name="p0")
-        nc.sync.dma_start(out=p0[:], in_=pos_embed[0:1, :].broadcast_to([32, HID]))
-
         for t in range(3, 6):
             load_x(t)
 
         ident = keep.tile([P, P], F32, name="ident")
         make_identity(nc, ident[:])
-        cls = keep.tile([32, HID], F32, name="cls")
 
         perm = []
         for i in range(3):
             pm = keep.tile([P, P], F32, name="perm%d" % i)
-            eng = nc.vector if i == 0 else nc.gpsimd
             for n, j in enumerate(order_of(i)):
-                eng.tensor_copy(out=pm[:, 8 * n:8 * n + 8], in_=ident[:, 8 * j:8 * j + 8])
+                nc.vector.tensor_copy(out=pm[:, 8 * n:8 * n + 8], in_=ident[:, 8 * j:8 * j + 8])
             perm.append(pm)
-        nc.gpsimd.tensor_tensor(out=cls[:], in0=ct[:], in1=p0[:], op=MULT)
 
         wc = {}
         ws = {}
@@ -117,6 +116,15 @@ def tile_myvit_kernel(tc, X, W, b, class_token, pos_embed, out):
         rgs, wrgs, grs, wgrs, xcs, xss = {}, {}, {}, {}, {}, {}
         free = list(range(8))
         count = {"t": 0}
+
+        spread = []
+        for r in range(3):
+            sp = psum.tile([P, HID], F32, name="spread%d" % r, tag="bk%d" % free.pop(0))
+            nc.tensor.matmul(out=sp[:], lhsT=ones[:], rhs=rows[r][:], start=True, stop=True)
+            spread.append(sp)
+        bias = keep.tile([P, HID], BF16, name="bias")
+        ct = keep.tile([P, HID], F32, name="ct")
+        cls = keep.tile([P, HID], F32, name="cls")
 
         def t_bank():
             k = free.pop(0)
@@ -251,7 +259,11 @@ def tile_myvit_kernel(tc, X, W, b, class_token, pos_embed, out):
 
         regroup(0, 10)
         regroup_rest(0)
+        nc.scalar.copy(out=bias[:], in_=spread[0][:])
+        nc.scalar.copy(out=ct[:], in_=spread[1][:])
         regroup_w(0, 0)
+        nc.vector.tensor_tensor(out=cls[:], in0=spread[2][:], in1=ct[:], op=MULT)
+        free.extend(range(3))
         transpose_x(0, (2,))
         regroup_w(1, 0)
         regroup_w(2, 0)
@@ -299,7 +311,7 @@ def tile_myvit_kernel(tc, X, W, b, class_token, pos_embed, out):
             quant_x(t)
             if k == 2:
                 quant_w(2, 1)
-                nc.sync.dma_start(out=out[:, 0, :], in_=cls[:])
+                nc.sync.dma_start(out=out[:, 0, :], in_=cls[0:32, :])
         times_pos(2)
         mx_passes(SEQ[-1])
         times_pos(1, nc.gpsimd)

@@ -58,13 +58,23 @@ def tile_myvit_kernel(tc, X, W, b, class_token, pos_embed, out):
         psum = ctx.enter_context(tc.psum_pool(name="psum", bufs=1))
 
         ones = keep.tile([P, P], BF16, name="ones")
-        nc.gpsimd.memset(ones[:], 1.0)
+        nc.vector.memset(ones[:], 1.0)
         rows = []
         for r, src in enumerate((b.rearrange("(o h) -> o h", o=1), class_token, pos_embed[0:1, :])):
             row = keep.tile([P, HID], BF16, name="row%d" % r)
-            nc.gpsimd.memset(row[:], 0.0)
+            nc.vector.memset(row[:], 0.0)
             nc.scalar.dma_start(out=row[0:1, :], in_=src)
             rows.append(row)
+        ident = keep.tile([P, P], F32, name="ident")
+        make_identity(nc, ident[:])
+
+        perm = []
+        for i in range(3):
+            pm = keep.tile([P, P], F32, name="perm%d" % i)
+            for n, j in enumerate(order_of(i)):
+                nc.vector.tensor_copy(out=pm[:, 8 * n:8 * n + 8], in_=ident[:, 8 * j:8 * j + 8])
+            perm.append(pm)
+
         pos = keep.tile([P, HID], BF16, name="pos")
 
         raws, wraws = {}, {}
@@ -90,20 +100,10 @@ def tile_myvit_kernel(tc, X, W, b, class_token, pos_embed, out):
         load_x(1)
         for c in range(3):
             load_w(c, 1)
-        for e in range(2):
-            nc.sync.dma_start(out=pos[64 * e:64 * e + 64, :], in_=pos_embed[1:65, :])
         for t in range(3, 6):
             load_x(t)
-
-        ident = keep.tile([P, P], F32, name="ident")
-        make_identity(nc, ident[:])
-
-        perm = []
-        for i in range(3):
-            pm = keep.tile([P, P], F32, name="perm%d" % i)
-            for n, j in enumerate(order_of(i)):
-                nc.vector.tensor_copy(out=pm[:, 8 * n:8 * n + 8], in_=ident[:, 8 * j:8 * j + 8])
-            perm.append(pm)
+        for e in range(2):
+            nc.sync.dma_start(out=pos[64 * e:64 * e + 64, :], in_=pos_embed[1:65, :])
 
         wc = {}
         ws = {}
@@ -251,7 +251,7 @@ def tile_myvit_kernel(tc, X, W, b, class_token, pos_embed, out):
 
         def times_pos(n, eng=nc.vector):
             for tmp, b0 in to_mul[:n]:
-                ost = outp.tile([P, HID], F32, name="ost%d" % b0, tag="ost")
+                ost = outp.tile([P, HID], F32, name="ost%d" % b0, tag="ost", bufs=6)
                 eng.tensor_tensor(out=ost[:], in0=tmp[:], in1=pos[:], op=MULT)
                 for e in range(2):
                     nc.sync.dma_start(out=out[b0 + e, 1:65, :], in_=ost[64 * e:64 * e + 64, :])

@@ -51,7 +51,7 @@ def tile_myvit_kernel(tc, X, W, b, class_token, pos_embed, out):
     with ExitStack() as ctx:
         ctx.enter_context(tc.manual_schedule())
         keep = ctx.enter_context(tc.tile_pool(name="keep", bufs=1))
-        rawp = ctx.enter_context(tc.tile_pool(name="rawp", bufs=6))
+        rawp = ctx.enter_context(tc.tile_pool(name="rawp", bufs=5))
         work = ctx.enter_context(tc.tile_pool(name="work", bufs=2))
         codes = ctx.enter_context(tc.tile_pool(name="codes", bufs=4))
         outp = ctx.enter_context(tc.tile_pool(name="outp", bufs=4))
@@ -100,7 +100,7 @@ def tile_myvit_kernel(tc, X, W, b, class_token, pos_embed, out):
         load_x(1)
         for c in range(3):
             load_w(c, 1)
-        for t in range(3, 6):
+        for t in range(3, 5):
             load_x(t)
         for e in range(2):
             nc.sync.dma_start(out=pos[64 * e:64 * e + 64, :], in_=pos_embed[1:65, :])
@@ -117,11 +117,13 @@ def tile_myvit_kernel(tc, X, W, b, class_token, pos_embed, out):
         free = list(range(8))
         count = {"t": 0}
 
-        spread = []
-        for r in range(3):
-            sp = psum.tile([P, HID], F32, name="spread%d" % r, tag="bk%d" % free.pop(0))
+        def spread(r):
+            k = free.pop(0)
+            free.append(k)
+            sp = psum.tile([P, HID], F32, name="spread%d" % r, tag="bk%d" % k)
             nc.tensor.matmul(out=sp[:], lhsT=ones[:], rhs=rows[r][:], start=True, stop=True)
-            spread.append(sp)
+            return sp
+
         bias = keep.tile([P, HID], BF16, name="bias")
         ct = keep.tile([P, HID], F32, name="ct")
         cls = keep.tile([P, HID], F32, name="cls")
@@ -133,7 +135,7 @@ def tile_myvit_kernel(tc, X, W, b, class_token, pos_embed, out):
             return psum.tile([P, 4, P], F32, name="tp%d" % count["t"], tag="bk%d" % k)
 
         def regroup(t, nv):
-            rg = work.tile([P, 4096], BF16, name="rg%d" % t, tag="rg")
+            rg = work.tile([P, 4096], BF16, name="rg%d" % t, tag="rg", bufs=3)
             o = rg[:].bitcast(F32).rearrange("p (g y w) -> p g y w", g=16, w=8)
             i = raws[t][:].bitcast(F32).rearrange("p (y g w) -> p g y w", g=16, w=8)
             nc.vector.tensor_copy(out=o[:, 0:nv, :, :], in_=i[:, 0:nv, :, :])
@@ -259,59 +261,67 @@ def tile_myvit_kernel(tc, X, W, b, class_token, pos_embed, out):
 
         regroup(0, 10)
         regroup_rest(0)
-        nc.scalar.copy(out=bias[:], in_=spread[0][:])
-        nc.scalar.copy(out=ct[:], in_=spread[1][:])
+        load_x(5)
         regroup_w(0, 0)
-        nc.vector.tensor_tensor(out=cls[:], in0=spread[2][:], in1=ct[:], op=MULT)
-        free.extend(range(3))
-        transpose_x(0, (2,))
         regroup_w(1, 0)
+        transpose_x(0, (2, 3))
         regroup_w(2, 0)
-        transpose_w(0, 0, ())
-        regroup(2, 10)
         quant_x(0)
-        transpose_w(1, 0, (1,))
-        regroup_rest(2)
+        transpose_w(0, 0, ())
         quant_w(0, 0)
-        transpose_w(2, 0, ())
-        regroup(1, 10)
+        regroup(2, 10)
+        transpose_w(1, 0, ())
         quant_w(1, 0)
-        quant_w(2, 0)
+        transpose_w(2, 0, (1,))
+        regroup_rest(2)
         load_x(6)
+        quant_w(2, 0)
+        regroup(1, 10)
         for k in range(1, NCHUNK):
             t = SEQ[k]
             nxt = SEQ[k + 1] if k + 1 < NCHUNK else None
             started = len(to_add)
             add_bias(started)
-            if nxt is not None and k > 1:
-                regroup(nxt, 10)
-            if t + 6 < NCHUNK:
-                load_x(t + 6)
-            transpose_x(t, (1, 3) if k == NCHUNK - 1 else ())
+            transpose_x(t, (3,) if k == NCHUNK - 1 else ())
             if k == 1:
                 regroup_rest(1)
+                load_x(7)
                 regroup_w(0, 1)
             if k == 2:
                 regroup_w(1, 1)
-                transpose_w(0, 1, ())
                 regroup_w(2, 1)
+                transpose_w(0, 1, ())
+                transpose_w(1, 1, (1,))
+                regroup(SEQ[3], 10)
             if nxt is not None:
                 times_pos(1)
             mx_passes(SEQ[k - 1])
+            if k == 1:
+                nc.scalar.copy(out=bias[:], in_=spread(0)[:])
+            if k == 4:
+                nc.scalar.copy(out=ct[:], in_=spread(1)[:])
             if k == 2:
-                transpose_w(1, 1, (1,))
                 quant_w(0, 1)
                 transpose_w(2, 1, (1,))
                 quant_w(1, 1)
             if started == 0:
                 times_pos(2)
             add_bias(1)
-            if nxt is not None and k > 1:
-                regroup_rest(nxt)
+            if k == 2:
+                regroup_rest(SEQ[3])
+                load_x(8)
             quant_x(t)
             if k == 2:
                 quant_w(2, 1)
+            if k == 4:
+                nc.vector.tensor_tensor(out=cls[:], in0=spread(2)[:], in1=ct[:], op=MULT)
                 nc.sync.dma_start(out=out[:, 0, :], in_=cls[0:32, :])
+            if k >= 2 and k + 2 < NCHUNK:
+                regroup(SEQ[k + 2], 10)
+                for n in () if k == 2 else ((4, 5) if k == 3 else (k + 2,)):
+                    regroup_rest(SEQ[n])
+                    if n + 5 < NCHUNK:
+                        load_x(n + 5)
         times_pos(2)
         mx_passes(SEQ[-1])
         times_pos(1, nc.gpsimd)

@@ -59,12 +59,13 @@ def tile_myvit_kernel(tc, X, W, b, class_token, pos_embed, out):
 
         ones = keep.tile([P, P], BF16, name="ones")
         nc.vector.memset(ones[:], 1.0)
-        rows = []
-        for r, src in enumerate((b.rearrange("(o h) -> o h", o=1), class_token, pos_embed[0:1, :])):
-            row = keep.tile([P, HID], BF16, name="row%d" % r)
-            nc.vector.memset(row[:], 0.0)
-            nc.scalar.dma_start(out=row[0:1, :], in_=src)
-            rows.append(row)
+        row = keep.tile([P, HID], BF16, name="row")
+        nc.vector.memset(row[:], 0.0)
+        nc.scalar.dma_start(out=row[0:1, :], in_=b.rearrange("(o h) -> o h", o=1))
+        bias = keep.tile([P, HID], BF16, name="bias")
+        ct = keep.tile([32, HID], BF16, name="ct")
+        p0 = keep.tile([32, HID], BF16, name="p0")
+        cls = keep.tile([32, HID], F32, name="cls")
         ident = keep.tile([P, P], F32, name="ident")
         make_identity(nc, ident[:])
 
@@ -117,16 +118,12 @@ def tile_myvit_kernel(tc, X, W, b, class_token, pos_embed, out):
         free = list(range(8))
         count = {"t": 0}
 
-        def spread(r):
+        def spread_bias():
             k = free.pop(0)
             free.append(k)
-            sp = psum.tile([P, HID], F32, name="spread%d" % r, tag="bk%d" % k)
-            nc.tensor.matmul(out=sp[:], lhsT=ones[:], rhs=rows[r][:], start=True, stop=True)
-            return sp
-
-        bias = keep.tile([P, HID], BF16, name="bias")
-        ct = keep.tile([P, HID], F32, name="ct")
-        cls = keep.tile([P, HID], F32, name="cls")
+            sp = psum.tile([P, HID], F32, name="spread", tag="bk%d" % k)
+            nc.tensor.matmul(out=sp[:], lhsT=ones[:], rhs=row[:], start=True, stop=True)
+            nc.scalar.copy(out=bias[:], in_=sp[:])
 
         def t_bank():
             k = free.pop(0)
@@ -224,39 +221,41 @@ def tile_myvit_kernel(tc, X, W, b, class_token, pos_embed, out):
             m, a = divmod(t, 2)
             i = m % 3
             for pair in range(WIN[i] // 6, WIN[i + 1] // 6):
-                if a == 0:
-                    k = free.pop(0)
-                    acc = psum.tile([P, HID], F32, name="acc%d_%d" % (m, pair), tag="bk%d" % k)
-                    accs[(m, pair)] = (acc, k)
-                acc, k = accs[(m, pair)]
-                for c in range(3):
-                    s0 = (6 * pair + 2 * c - WIN[i]) * 64
-                    nc.tensor.matmul_mx(
-                        out=acc[:],
-                        lhsT=xcs[t][:, s0:s0 + P].bitcast(FP8X4),
-                        lhsT_scale=xss[t][:, s0:s0 + P],
-                        rhs=wc[(c, a)][:].bitcast(FP8X4),
-                        rhs_scale=ws[(c, a)][:],
-                        start=(a == 0 and c == 0),
-                        stop=(a == 1 and c == 2),
-                    )
-                if a == 1:
-                    to_add.append((acc, k, 16 * (m // 3) + 2 * pair))
+                width = HID // 2 if m == NCHUNK // 2 - 1 and pair == 7 else HID
+                for h0 in range(0, HID, width):
+                    if a == 0:
+                        k = free.pop(0)
+                        acc = psum.tile([P, width], F32, name="acc%d_%d_%d" % (m, pair, h0), tag="bk%d" % k)
+                        accs[(m, pair, h0)] = (acc, k)
+                    acc, k = accs[(m, pair, h0)]
+                    for c in range(3):
+                        s0 = (6 * pair + 2 * c - WIN[i]) * 64
+                        nc.tensor.matmul_mx(
+                            out=acc[:],
+                            lhsT=xcs[t][:, s0:s0 + P].bitcast(FP8X4),
+                            lhsT_scale=xss[t][:, s0:s0 + P],
+                            rhs=wc[(c, a)][:, h0:h0 + width].bitcast(FP8X4),
+                            rhs_scale=ws[(c, a)][:, h0:h0 + width],
+                            start=(a == 0 and c == 0),
+                            stop=(a == 1 and c == 2),
+                        )
+                    if a == 1:
+                        to_add.append((acc, k, 16 * (m // 3) + 2 * pair, slice(h0, h0 + width)))
 
         def add_bias(n):
-            for acc, k, b0 in to_add[:n]:
+            for acc, k, b0, cols in to_add[:n]:
                 free.append(k)
-                tmp = outp.tile([P, HID], F32, name="tmp%d" % b0, tag="tmp")
-                nc.vector.tensor_tensor(out=tmp[:], in0=acc[:], in1=bias[:], op=ADD)
-                to_mul.append((tmp, b0))
+                tmp = outp.tile([P, HID], F32, name="tmp%d_%d" % (b0, cols.start), tag="tmp")
+                nc.vector.tensor_tensor(out=tmp[:, cols], in0=acc[:], in1=bias[:, cols], op=ADD)
+                to_mul.append((tmp, b0, cols))
             to_add[:n] = []
 
         def times_pos(n, eng=nc.vector):
-            for tmp, b0 in to_mul[:n]:
-                ost = outp.tile([P, HID], F32, name="ost%d" % b0, tag="ost", bufs=6)
-                eng.tensor_tensor(out=ost[:], in0=tmp[:], in1=pos[:], op=MULT)
+            for tmp, b0, cols in to_mul[:n]:
+                ost = outp.tile([P, HID], F32, name="ost%d_%d" % (b0, cols.start), tag="ost", bufs=6)
+                eng.tensor_tensor(out=ost[:, cols], in0=tmp[:, cols], in1=pos[:, cols], op=MULT)
                 for e in range(2):
-                    nc.sync.dma_start(out=out[b0 + e, 1:65, :], in_=ost[64 * e:64 * e + 64, :])
+                    nc.sync.dma_start(out=out[b0 + e, 1:65, cols], in_=ost[64 * e:64 * e + 64, cols])
             to_mul[:n] = []
 
         regroup(0, 10)
@@ -297,9 +296,7 @@ def tile_myvit_kernel(tc, X, W, b, class_token, pos_embed, out):
                 times_pos(1)
             mx_passes(SEQ[k - 1])
             if k == 1:
-                nc.scalar.copy(out=bias[:], in_=spread(0)[:])
-            if k == 4:
-                nc.scalar.copy(out=ct[:], in_=spread(1)[:])
+                spread_bias()
             if k == 2:
                 quant_w(0, 1)
                 transpose_w(2, 1, (1,))
@@ -313,9 +310,12 @@ def tile_myvit_kernel(tc, X, W, b, class_token, pos_embed, out):
             quant_x(t)
             if k == 2:
                 quant_w(2, 1)
-            if k == 4:
-                nc.vector.tensor_tensor(out=cls[:], in0=spread(2)[:], in1=ct[:], op=MULT)
-                nc.sync.dma_start(out=out[:, 0, :], in_=cls[0:32, :])
+            if k == 5:
+                nc.sync.dma_start(out=ct[:], in_=class_token.broadcast_to([32, HID]))
+                nc.sync.dma_start(out=p0[:], in_=pos_embed[0:1, :].broadcast_to([32, HID]))
+            if k == 9:
+                nc.vector.tensor_tensor(out=cls[:], in0=ct[:], in1=p0[:], op=MULT)
+                nc.sync.dma_start(out=out[:, 0, :], in_=cls[:])
             if k >= 2 and k + 2 < NCHUNK:
                 regroup(SEQ[k + 2], 10)
                 for n in () if k == 2 else ((4, 5) if k == 3 else (k + 2,)):
@@ -328,4 +328,6 @@ def tile_myvit_kernel(tc, X, W, b, class_token, pos_embed, out):
         add_bias(1)
         times_pos(1, nc.gpsimd)
         add_bias(2)
+        times_pos(1)
+        add_bias(1)
         times_pos(2)

from contextlib import ExitStack

import concourse.mybir as mybir
from concourse.masks import make_identity

F32 = mybir.dt.float32
BF16 = mybir.dt.bfloat16
U32 = mybir.dt.uint32
U8 = mybir.dt.uint8
FP8X4 = mybir.dt.float8_e4m3fn_x4
ADD = mybir.AluOpType.add
MULT = mybir.AluOpType.mult

P = 128
HID = 512
NCHUNK = 12
OCT = 16
SLOTW = 128
WIN = (0, 12, 30, 48)
FLOPS = 2 * 2048 * 3072 * 512


def place(j):
    pair, r = divmod(j, 6)
    e, c = divmod(r, 3)
    return 6 * pair + 2 * c + e


def order_of(i):
    return sorted(range(OCT), key=lambda j: place(OCT * i + j))


def runs_of(i):
    places = [place(OCT * i + j) for j in order_of(i)]
    out = []
    for n, s in enumerate(places):
        nxt = s >= WIN[i + 1]
        rel = s - (WIN[i + 1] if nxt else WIN[i])
        if out and out[-1][1] == nxt:
            q0, x, first, count, step = out[-1]
            d = rel - (first + (count - 1) * step)
            if count == 1 or d == step:
                out[-1] = (q0, x, first, count + 1, d)
                continue
        out.append((8 * n, nxt, rel, 1, 1))
    return out


def tile_myvit_kernel(tc, X, W, b, class_token, pos_embed, out):
    nc = tc.nc
    with ExitStack() as ctx:
        ctx.enter_context(tc.manual_schedule())
        keep = ctx.enter_context(tc.tile_pool(name="keep", bufs=1))
        rawp = ctx.enter_context(tc.tile_pool(name="rawp", bufs=5))
        work = ctx.enter_context(tc.tile_pool(name="work", bufs=2))
        codes = ctx.enter_context(tc.tile_pool(name="codes", bufs=4))
        outp = ctx.enter_context(tc.tile_pool(name="outp", bufs=4))
        psum = ctx.enter_context(tc.psum_pool(name="psum", bufs=1))

        ones = keep.tile([P, P], BF16, name="ones")
        nc.vector.memset(ones[:], 1.0)
        row = keep.tile([P, HID], BF16, name="row")
        nc.vector.memset(row[:], 0.0)
        nc.scalar.dma_start(out=row[0:1, :], in_=b.rearrange("(o h) -> o h", o=1))
        bias = keep.tile([P, HID], BF16, name="bias")
        ct = keep.tile([32, HID], BF16, name="ct")
        p0 = keep.tile([32, HID], BF16, name="p0")
        cls = keep.tile([32, HID], F32, name="cls")
        ident = keep.tile([P, P], F32, name="ident")
        make_identity(nc, ident[:])

        perm = []
        for i in range(3):
            pm = keep.tile([P, P], F32, name="perm%d" % i)
            for n, j in enumerate(order_of(i)):
                nc.vector.tensor_copy(out=pm[:, 8 * n:8 * n + 8], in_=ident[:, 8 * j:8 * j + 8])
            perm.append(pm)

        pos = keep.tile([P, HID], BF16, name="pos")

        raws, wraws = {}, {}
        x_rows = X.rearrange("b c (g a y) x -> (b c g) a (y x)", g=8, a=2)
        w_view = W.rearrange("(t p) (c a k) -> c a p t k", p=P, c=3, a=2)

        def load_x(t):
            m, a = divmod(t, 2)
            raw = rawp.tile([P, 4096], BF16, name="raw%d" % t, tag="raw")
            nc.sync.dma_start(out=raw[:], in_=x_rows[m * P:(m + 1) * P, a, :])
            raws[t] = raw

        def load_w(c, a):
            wr = keep.tile([P, 4, 512], BF16, name="wraw%d%d" % (c, a))
            nc.sync.dma_start(out=wr[:], in_=w_view[c, a])
            wraws[(c, a)] = wr

        SEQ = [0, 2, 1] + list(range(3, NCHUNK))
        load_x(0)
        for c in range(3):
            load_w(c, 0)
        load_x(2)
        load_x(1)
        for c in range(3):
            load_w(c, 1)
        for t in range(3, 5):
            load_x(t)
        for e in range(2):
            nc.sync.dma_start(out=pos[64 * e:64 * e + 64, :], in_=pos_embed[1:65, :])

        wc = {}
        ws = {}
        for a in range(2):
            for c in range(3):
                wcode = keep.tile([P, HID], U32, name="wc%d%d" % (c, a), align_bytes=64)
                wscale = keep.tile([P, HID], U8, name="ws%d%d" % (c, a), align_bytes=64)
                wc[(c, a)], ws[(c, a)] = wcode, wscale

        rgs, wrgs, grs, wgrs, xcs, xss = {}, {}, {}, {}, {}, {}
        free = list(range(8))
        count = {"t": 0}

        def spread_bias():
            k = free.pop(0)
            free.append(k)
            sp = psum.tile([P, HID], F32, name="spread", tag="bk%d" % k)
            nc.tensor.matmul(out=sp[:], lhsT=ones[:], rhs=row[:], start=True, stop=True)
            nc.scalar.copy(out=bias[:], in_=sp[:])

        def t_bank():
            k = free.pop(0)
            free.append(k)
            count["t"] += 1
            return psum.tile([P, 4, P], F32, name="tp%d" % count["t"], tag="bk%d" % k)

        def regroup(t, nv):
            rg = work.tile([P, 4096], BF16, name="rg%d" % t, tag="rg", bufs=3)
            o = rg[:].bitcast(F32).rearrange("p (g y w) -> p g y w", g=16, w=8)
            i = raws[t][:].bitcast(F32).rearrange("p (y g w) -> p g y w", g=16, w=8)
            nc.vector.tensor_copy(out=o[:, 0:nv, :, :], in_=i[:, 0:nv, :, :])
            rgs[t] = (rg, o, i, nv)

        def regroup_rest(t):
            rg, o, i, nv = rgs[t]
            if nv < 16:
                nc.scalar.copy(out=o[:, nv:16, :, :], in_=i[:, nv:16, :, :])

        def regroup_w(c, a):
            wrg = work.tile([P, 2048], BF16, name="wrg%d%d" % (c, a), tag="wrg", bufs=3)
            for u in range(2):
                nc.vector.tensor_copy(
                    out=wrg[:].bitcast(F32).rearrange("p (t u y w) -> p t u y w", t=4, u=2, w=8)[:, :, u, :, :],
                    in_=wraws[(c, a)][:].rearrange("p t k -> p (t k)").bitcast(F32).rearrange("p (t y u w) -> p t y u w", t=4, u=2, w=8)[:, :, :, u, :],
                )
            wrgs[(c, a)] = wrg

        def gr_tile(t):
            if t not in grs and t < NCHUNK:
                gr = work.tile([P, 18 * 2 * SLOTW], BF16, name="gr%d" % t, tag="gr%d" % (t % 2), bufs=3, align_bytes=64)
                grs[t] = gr

        def transpose_x(t, vector_banks=()):
            i = (t // 2) % 3
            gr_tile(t)
            if i < 2:
                gr_tile(t + 2)
            rgf = rgs[t][0][:].bitcast(F32)
            for j in range(4):
                bank = t_bank()
                for v in range(4):
                    k0 = (4 * j + v) * P
                    nc.tensor.transpose(out=bank[:, v, :], in_=rgf[:, k0:k0 + P], identity=perm[i][:])
                for q0, nxt, first, count, step in runs_of(i):
                    gr = grs[t + 2 if nxt else t]
                    dst = gr[:].bitcast(F32).rearrange("p (s q w) -> p s q w", q=8, w=16)
                    dst = dst[:, first:first + (count - 1) * step + 1:step, :, 4 * j:4 * j + 4]
                    src = bank[:, :, q0:q0 + 8 * count].rearrange("p v (s q) -> p s q v", q=8)
                    if j in vector_banks:
                        nc.vector.tensor_copy(out=dst, in_=src)
                    else:
                        nc.scalar.copy(out=dst, in_=src)

        def transpose_w(c, a, vector_banks):
            wgr = work.tile([P, 2048], BF16, name="wgr%d%d" % (c, a), tag="wgr", bufs=3, align_bytes=64)
            wgrf = wgr[:].bitcast(F32).rearrange("p (t h u) -> p t h u", t=4, u=2)
            src = wrgs[(c, a)][:].bitcast(F32)
            for j in range(2):
                bank = t_bank()
                for v in range(4):
                    k0 = (4 * j + v) * P
                    nc.tensor.transpose(out=bank[:, v, :], in_=src[:, k0:k0 + P], identity=ident[:])
                copy = nc.vector.tensor_copy if j in vector_banks else nc.scalar.copy
                copy(out=wgrf[:, 2 * j:2 * j + 2, :, :], in_=bank[:].rearrange("p (t u) h -> p t h u", u=2))
            wgrs[(c, a)] = wgr

        def quant_w(c, a):
            nc.vector.quantize_mx(out=wc[(c, a)][:].bitcast(FP8X4), scales=ws[(c, a)][:], in_=wgrs[(c, a)][:])

        def quant_x(t):
            i = (t // 2) % 3
            n = WIN[i + 1] - WIN[i]
            xc = codes.tile([P, 18 * 64], U32, name="xc%d" % t, tag="xc", align_bytes=64)
            xs = codes.tile([P, 18 * 64], U8, name="xs%d" % t, tag="xs", align_bytes=64)
            xcs[t], xss[t] = xc, xs
            s = 0
            while s < n:
                k = 8
                while s + k > n:
                    k //= 2
                if t < NCHUNK - 1 and s + 16 <= n:
                    k = 16
                nc.vector.quantize_mx(
                    out=xc[:, s * 64:(s + k) * 64].bitcast(FP8X4),
                    scales=xs[:, s * 64:(s + k) * 64],
                    in_=grs[t][:, s * 256:(s + k) * 256],
                )
                s += k

        accs = {}
        to_add, to_mul = [], []

        def mx_passes(t):
            m, a = divmod(t, 2)
            i = m % 3
            for pair in range(WIN[i] // 6, WIN[i + 1] // 6):
                width = HID // 2 if m == NCHUNK // 2 - 1 and pair == 7 else HID
                for h0 in range(0, HID, width):
                    if a == 0:
                        k = free.pop(0)
                        acc = psum.tile([P, width], F32, name="acc%d_%d_%d" % (m, pair, h0), tag="bk%d" % k)
                        accs[(m, pair, h0)] = (acc, k)
                    acc, k = accs[(m, pair, h0)]
                    for c in range(3):
                        s0 = (6 * pair + 2 * c - WIN[i]) * 64
                        nc.tensor.matmul_mx(
                            out=acc[:],
                            lhsT=xcs[t][:, s0:s0 + P].bitcast(FP8X4),
                            lhsT_scale=xss[t][:, s0:s0 + P],
                            rhs=wc[(c, a)][:, h0:h0 + width].bitcast(FP8X4),
                            rhs_scale=ws[(c, a)][:, h0:h0 + width],
                            start=(a == 0 and c == 0),
                            stop=(a == 1 and c == 2),
                        )
                    if a == 1:
                        to_add.append((acc, k, 16 * (m // 3) + 2 * pair, slice(h0, h0 + width)))

        def add_bias(n):
            for acc, k, b0, cols in to_add[:n]:
                free.append(k)
                tmp = outp.tile([P, HID], F32, name="tmp%d_%d" % (b0, cols.start), tag="tmp")
                nc.vector.tensor_tensor(out=tmp[:, cols], in0=acc[:], in1=bias[:, cols], op=ADD)
                to_mul.append((tmp, b0, cols))
            to_add[:n] = []

        def times_pos(n, eng=nc.vector):
            for tmp, b0, cols in to_mul[:n]:
                ost = outp.tile([P, HID], F32, name="ost%d_%d" % (b0, cols.start), tag="ost", bufs=6)
                eng.tensor_tensor(out=ost[:, cols], in0=tmp[:, cols], in1=pos[:, cols], op=MULT)
                for e in range(2):
                    nc.sync.dma_start(out=out[b0 + e, 1:65, cols], in_=ost[64 * e:64 * e + 64, cols])
            to_mul[:n] = []

        regroup(0, 10)
        regroup_rest(0)
        load_x(5)
        regroup_w(0, 0)
        regroup_w(1, 0)
        transpose_x(0, (2, 3))
        regroup_w(2, 0)
        quant_x(0)
        transpose_w(0, 0, ())
        quant_w(0, 0)
        regroup(2, 10)
        transpose_w(1, 0, ())
        quant_w(1, 0)
        transpose_w(2, 0, (1,))
        regroup_rest(2)
        load_x(6)
        quant_w(2, 0)
        regroup(1, 10)
        for k in range(1, NCHUNK):
            t = SEQ[k]
            nxt = SEQ[k + 1] if k + 1 < NCHUNK else None
            started = len(to_add)
            add_bias(started)
            transpose_x(t, (3,) if k == NCHUNK - 1 else ())
            if k == 1:
                regroup_rest(1)
                load_x(7)
                regroup_w(0, 1)
            if k == 2:
                regroup_w(1, 1)
                regroup_w(2, 1)
                transpose_w(0, 1, ())
                transpose_w(1, 1, (1,))
                regroup(SEQ[3], 10)
            if nxt is not None:
                times_pos(1)
            mx_passes(SEQ[k - 1])
            if k == 1:
                spread_bias()
            if k == 2:
                quant_w(0, 1)
                transpose_w(2, 1, (1,))
                quant_w(1, 1)
            if started == 0:
                times_pos(2)
            add_bias(1)
            if k == 2:
                regroup_rest(SEQ[3])
                load_x(8)
            quant_x(t)
            if k == 2:
                quant_w(2, 1)
            if k == 5:
                nc.sync.dma_start(out=ct[:], in_=class_token.broadcast_to([32, HID]))
                nc.sync.dma_start(out=p0[:], in_=pos_embed[0:1, :].broadcast_to([32, HID]))
            if k == 9:
                nc.vector.tensor_tensor(out=cls[:], in0=ct[:], in1=p0[:], op=MULT)
                nc.sync.dma_start(out=out[:, 0, :], in_=cls[:])
            if k >= 2 and k + 2 < NCHUNK:
                regroup(SEQ[k + 2], 10)
                for n in () if k == 2 else ((4, 5) if k == 3 else (k + 2,)):
                    regroup_rest(SEQ[n])
                    if n + 5 < NCHUNK:
                        load_x(n + 5)
        times_pos(2)
        mx_passes(SEQ[-1])
        times_pos(1, nc.gpsimd)
        add_bias(1)
        times_pos(1, nc.gpsimd)
        add_bias(2)
        times_pos(1)
        add_bias(1)
        times_pos(2)
